import numpy as np
import ml_dtypes

BF16 = ml_dtypes.bfloat16


def bf(x):
    return np.asarray(x, np.float32).astype(BF16)


def f32(x):
    return np.asarray(x, np.float32)


def f64(x):
    return np.asarray(x).astype(np.float64)


def striped(idx):
    return np.tile(idx.reshape(-1, 16).T, (8, 1))


E, H, Q, S, N = 256, 512, 4, 512, 128


def sigmoid(v):
    return 1.0 / (1.0 + np.exp(-v))


def setup_inputs():
    return {"base": f32(0.3 * np.random.standard_normal((H, S))), "x0": bf(np.random.standard_normal((E + H, N))), "h": bf(np.random.standard_normal((H, N))), "cell": f32(np.random.standard_normal((H, N))), "wi": bf(np.random.standard_normal((E + H, Q * H)) / np.sqrt(E + H)), "wh": bf(np.random.standard_normal((H, Q * H)) / np.sqrt(H)), "b": f32(0.3 * np.random.standard_normal((Q * H, 1))), "offs": striped(np.random.permutation(S)[:N])}


def reference(base, x0, h, cell, wi, wh, b, offs):
    idx = offs[:16].T.reshape(-1)
    z = f64(wi).T @ f64(x0) + f64(wh).T @ f64(h) + f64(b)
    zi, zf, zu, zo = z.reshape(Q, H, N)
    cn = sigmoid(zf) * f64(cell) + sigmoid(zi) * np.tanh(zu)
    out = f64(base).copy()
    out[:, idx] = sigmoid(zo) * np.tanh(cn)
    return out

@@ -1,0 +1,105 @@
+import concourse.masks as masks
+import concourse.mybir as mybir
+
+BF16, F32, U16 = mybir.dt.bfloat16, mybir.dt.float32, mybir.dt.uint16
+SIGMOID = mybir.ActivationFunctionType.Sigmoid
+TANH = mybir.ActivationFunctionType.Tanh
+MULT, ADD = mybir.AluOpType.mult, mybir.AluOpType.add
+
+P = 128
+H = 512
+N = 128
+S = 512
+CB = H // P
+GATE_I, GATE_F, GATE_U, GATE_O = 0, 1, 2, 3
+EARLY = (GATE_I, GATE_F, GATE_U)
+
+FLOPS = 2 * (768 + 512) * 4 * H * N
+
+
+def tile_outputdecoder_kernel(tc, base, x0, h, cell, wi, wh, b, offs, out):
+    nc = tc.nc
+    with tc.tile_pool(name="held", bufs=1) as held, tc.psum_pool(name="psum", bufs=1) as psum:
+        offsets = held.tile([P, N // 16], U16, name="offsets")
+        nc.sync.dma_start(offsets[:], offs)
+
+        sources = []
+        for label, weights, moving in (("x", wi, x0), ("h", wh, h)):
+            blocks = moving.shape[0] // P
+            moving_sb = held.tile([P, blocks, N], BF16, name=f"moving_{label}")
+            nc.sync.dma_start(moving_sb[:], moving.rearrange("(p kb) j -> p kb j", kb=blocks))
+            weights_view = weights.rearrange("(p kb) m -> p kb m", kb=blocks)
+            for kb in range(blocks):
+                sources.append((weights_view[:, kb, :], moving_sb[:, kb, :]))
+        K_BLOCKS = len(sources)
+
+        bias_rows = held.tile([P, P], F32, name="bias_rows")
+        nc.vector.memset(bias_rows[:], 0.0)
+        nc.scalar.dma_start(bias_rows[0 : 4 * CB, :], b.rearrange("(r p) one -> r (p one)", p=P))
+
+        early_w = []
+        for kb, (weights_hbm, moving_block) in enumerate(sources):
+            early_w.append(held.tile([P, len(EARLY) * H], BF16, name=f"early_w{kb}"))
+            nc.sync.dma_start(early_w[kb][:], weights_hbm[:, 0 : len(EARLY) * H])
+        cell_sb = held.tile([P, CB, N], F32, name="cell_sb")
+        nc.sync.dma_start(cell_sb[:], cell.rearrange("(cb p) j -> p cb j", p=P))
+        late_w = []
+        for kb, (weights_hbm, moving_block) in enumerate(sources):
+            late_w.append(held.tile([P, H], BF16, name=f"late_w{kb}"))
+            nc.sync.dma_start(late_w[kb][:], weights_hbm[:, GATE_O * H : (GATE_O + 1) * H])
+        windows = []
+        for cb in range(CB):
+            windows.append(held.tile([P, S], F32, name=f"window{cb}"))
+            nc.sync.dma_start(windows[cb][:], base[cb * P : (cb + 1) * P, :])
+
+        identity = held.tile([P, P], F32, name="identity")
+        masks.make_identity(nc, identity[:])
+        bias_ps = psum.tile([P, P], F32, name="bias_ps")
+        nc.tensor.transpose(bias_ps[:], bias_rows[:], identity[:])
+        bias = held.tile([P, 4 * CB], F32, name="bias")
+        nc.vector.tensor_copy(bias[:], bias_ps[:, 0 : 4 * CB])
+
+        z = [psum.tile([P, CB, N], F32, name=f"z{gate}") for gate in range(4)]
+
+        def accumulate(gate, kb, weights_sb, first_column):
+            for cb in range(CB):
+                nc.tensor.matmul(
+                    z[gate][:, cb, :],
+                    weights_sb[:, first_column + cb * P : first_column + (cb + 1) * P],
+                    sources[kb][1],
+                    start=(kb == 0 and cb == 0),
+                    stop=(kb == K_BLOCKS - 1 and cb == CB - 1),
+                )
+
+        def squash(gate, cb, func, label):
+            squashed = held.tile([P, N], F32, name=f"{label}{cb}")
+            column = gate * CB + cb
+            nc.scalar.activation(squashed[:], z[gate][:, cb, :], func, bias=bias[:, column : column + 1])
+            return squashed
+
+        for kb in range(K_BLOCKS):
+            for gate in EARLY:
+                accumulate(gate, kb, early_w[kb], gate * H)
+
+        sig_i = [squash(GATE_I, cb, SIGMOID, "sig_i") for cb in range(CB)]
+        sig_f = [squash(GATE_F, cb, SIGMOID, "sig_f") for cb in range(CB)]
+        tanh_u = [squash(GATE_U, cb, TANH, "tanh_u") for cb in range(CB)]
+
+        tanh_cn = []
+        for cb in range(CB):
+            kept = held.tile([P, N], F32, name=f"kept{cb}")
+            nc.vector.tensor_tensor(kept[:], sig_f[cb][:], cell_sb[:, cb, :], MULT)
+            fresh = held.tile([P, N], F32, name=f"fresh{cb}")
+            nc.vector.tensor_tensor(fresh[:], sig_i[cb][:], tanh_u[cb][:], MULT)
+            cn = held.tile([P, N], F32, name=f"cn{cb}")
+            nc.vector.tensor_tensor(cn[:], kept[:], fresh[:], ADD)
+            tanh_cn.append(held.tile([P, N], F32, name=f"tanh_cn{cb}"))
+            nc.scalar.activation(tanh_cn[cb][:], cn[:], TANH)
+
+        for kb in range(K_BLOCKS):
+            accumulate(GATE_O, kb, late_w[kb], 0)
+
+        for cb in range(CB):
+            sig_o = squash(GATE_O, cb, SIGMOID, "sig_o")
+            nc.vector.tensor_tensor(windows[cb][:].indirect(offsets[:]), sig_o[:], tanh_cn[cb][:], MULT)
+            nc.sync.dma_start(out[cb * P : (cb + 1) * P, :], windows[cb][:])

@@ -13,6 +13,7 @@ S = 512
 CB = H // P
 GATE_I, GATE_F, GATE_U, GATE_O = 0, 1, 2, 3
 EARLY = (GATE_I, GATE_F, GATE_U)
+WARM_UPS = 6
 
 FLOPS = 2 * (768 + 512) * 4 * H * N
 
@@ -23,34 +24,42 @@ def tile_outputdecoder_kernel(tc, base, x0, h, cell, wi, wh, b, offs, out):
         offsets = held.tile([P, N // 16], U16, name="offsets")
         nc.sync.dma_start(offsets[:], offs)
 
-        sources = []
+        weights_hbm = []
+        moving_sb = []
         for label, weights, moving in (("x", wi, x0), ("h", wh, h)):
             blocks = moving.shape[0] // P
-            moving_sb = held.tile([P, blocks, N], BF16, name=f"moving_{label}")
-            nc.sync.dma_start(moving_sb[:], moving.rearrange("(p kb) j -> p kb j", kb=blocks))
+            moving_tile = held.tile([P, blocks, N], BF16, name=f"moving_{label}")
+            nc.sync.dma_start(moving_tile[:], moving.rearrange("(p kb) j -> p kb j", kb=blocks))
             weights_view = weights.rearrange("(p kb) m -> p kb m", kb=blocks)
             for kb in range(blocks):
-                sources.append((weights_view[:, kb, :], moving_sb[:, kb, :]))
-        K_BLOCKS = len(sources)
+                weights_hbm.append(weights_view[:, kb, :])
+                moving_sb.append(moving_tile[:, kb, :])
+        K_BLOCKS = len(weights_hbm)
 
         bias_rows = held.tile([P, P], F32, name="bias_rows")
         nc.vector.memset(bias_rows[:], 0.0)
         nc.scalar.dma_start(bias_rows[0 : 4 * CB, :], b.rearrange("(r p) one -> r (p one)", p=P))
 
         early_w = []
-        for kb, (weights_hbm, moving_block) in enumerate(sources):
+        for kb in range(K_BLOCKS):
             early_w.append(held.tile([P, len(EARLY) * H], BF16, name=f"early_w{kb}"))
-            nc.sync.dma_start(early_w[kb][:], weights_hbm[:, 0 : len(EARLY) * H])
+            nc.sync.dma_start(early_w[kb][:], weights_hbm[kb][:, 0 : len(EARLY) * H])
         cell_sb = held.tile([P, CB, N], F32, name="cell_sb")
         nc.sync.dma_start(cell_sb[:], cell.rearrange("(cb p) j -> p cb j", p=P))
         late_w = []
-        for kb, (weights_hbm, moving_block) in enumerate(sources):
+        for kb in range(K_BLOCKS):
             late_w.append(held.tile([P, H], BF16, name=f"late_w{kb}"))
-            nc.sync.dma_start(late_w[kb][:], weights_hbm[:, GATE_O * H : (GATE_O + 1) * H])
+            nc.sync.dma_start(late_w[kb][:], weights_hbm[kb][:, GATE_O * H : (GATE_O + 1) * H])
         windows = []
         for cb in range(CB):
             windows.append(held.tile([P, S], F32, name=f"window{cb}"))
             nc.sync.dma_start(windows[cb][:], base[cb * P : (cb + 1) * P, :])
+
+        zeros = held.tile([P, 512], BF16, name="zeros")
+        nc.vector.memset(zeros[:], 0.0)
+        unread = psum.tile([P, 512], F32, name="unread")
+        for warm_up in range(WARM_UPS):
+            nc.tensor.matmul(unread[:], zeros[:, 0:P], zeros[:], start=True, stop=True)
 
         identity = held.tile([P, P], F32, name="identity")
         masks.make_identity(nc, identity[:])
@@ -66,7 +75,7 @@ def tile_outputdecoder_kernel(tc, base, x0, h, cell, wi, wh, b, offs, out):
                 nc.tensor.matmul(
                     z[gate][:, cb, :],
                     weights_sb[:, first_column + cb * P : first_column + (cb + 1) * P],
-                    sources[kb][1],
+                    moving_sb[kb],
                     start=(kb == 0 and cb == 0),
                     stop=(kb == K_BLOCKS - 1 and cb == CB - 1),
                 )

@@ -13,7 +13,6 @@ S = 512
 CB = H // P
 GATE_I, GATE_F, GATE_U, GATE_O = 0, 1, 2, 3
 EARLY = (GATE_I, GATE_F, GATE_U)
-WARM_UPS = 6
 
 FLOPS = 2 * (768 + 512) * 4 * H * N
 
@@ -25,6 +24,7 @@ def tile_outputdecoder_kernel(tc, base, x0, h, cell, wi, wh, b, offs, out):
         nc.sync.dma_start(offsets[:], offs)
 
         weights_hbm = []
+        weights_hbm_pairs = []
         moving_sb = []
         for label, weights, moving in (("x", wi, x0), ("h", wh, h)):
             blocks = moving.shape[0] // P
@@ -34,6 +34,8 @@ def tile_outputdecoder_kernel(tc, base, x0, h, cell, wi, wh, b, offs, out):
             for kb in range(blocks):
                 weights_hbm.append(weights_view[:, kb, :])
                 moving_sb.append(moving_tile[:, kb, :])
+            for kb in range(0, blocks, 2):
+                weights_hbm_pairs.append(weights_view[:, kb : kb + 2, :])
         K_BLOCKS = len(weights_hbm)
 
         bias_rows = held.tile([P, P], F32, name="bias_rows")
@@ -43,23 +45,20 @@ def tile_outputdecoder_kernel(tc, base, x0, h, cell, wi, wh, b, offs, out):
         early_w = []
         for kb in range(K_BLOCKS):
             early_w.append(held.tile([P, len(EARLY) * H], BF16, name=f"early_w{kb}"))
-            nc.sync.dma_start(early_w[kb][:], weights_hbm[kb][:, 0 : len(EARLY) * H])
+            queue = nc.sync if kb % 2 == 0 else nc.scalar
+            queue.dma_start(early_w[kb][:], weights_hbm[kb][:, 0 : len(EARLY) * H])
         cell_sb = held.tile([P, CB, N], F32, name="cell_sb")
         nc.sync.dma_start(cell_sb[:], cell.rearrange("(cb p) j -> p cb j", p=P))
         late_w = []
-        for kb in range(K_BLOCKS):
-            late_w.append(held.tile([P, H], BF16, name=f"late_w{kb}"))
-            nc.sync.dma_start(late_w[kb][:], weights_hbm[kb][:, GATE_O * H : (GATE_O + 1) * H])
+        for pair, pair_hbm in enumerate(weights_hbm_pairs):
+            late_pair = held.tile([P, 2, H], BF16, name=f"late_pair{pair}")
+            nc.sync.dma_start(late_pair[:], pair_hbm[:, :, GATE_O * H : (GATE_O + 1) * H])
+            late_w.append(late_pair[:, 0, :])
+            late_w.append(late_pair[:, 1, :])
         windows = []
         for cb in range(CB):
             windows.append(held.tile([P, S], F32, name=f"window{cb}"))
             nc.sync.dma_start(windows[cb][:], base[cb * P : (cb + 1) * P, :])
-
-        zeros = held.tile([P, 512], BF16, name="zeros")
-        nc.vector.memset(zeros[:], 0.0)
-        unread = psum.tile([P, 512], F32, name="unread")
-        for warm_up in range(WARM_UPS):
-            nc.tensor.matmul(unread[:], zeros[:, 0:P], zeros[:], start=True, stop=True)
 
         identity = held.tile([P, P], F32, name="identity")
         masks.make_identity(nc, identity[:])

@@ -24,7 +24,6 @@ def tile_outputdecoder_kernel(tc, base, x0, h, cell, wi, wh, b, offs, out):
         nc.sync.dma_start(offsets[:], offs)
 
         weights_hbm = []
-        weights_hbm_pairs = []
         moving_sb = []
         for label, weights, moving in (("x", wi, x0), ("h", wh, h)):
             blocks = moving.shape[0] // P
@@ -34,8 +33,6 @@ def tile_outputdecoder_kernel(tc, base, x0, h, cell, wi, wh, b, offs, out):
             for kb in range(blocks):
                 weights_hbm.append(weights_view[:, kb, :])
                 moving_sb.append(moving_tile[:, kb, :])
-            for kb in range(0, blocks, 2):
-                weights_hbm_pairs.append(weights_view[:, kb : kb + 2, :])
         K_BLOCKS = len(weights_hbm)
 
         bias_rows = held.tile([P, P], F32, name="bias_rows")
@@ -45,16 +42,13 @@ def tile_outputdecoder_kernel(tc, base, x0, h, cell, wi, wh, b, offs, out):
         early_w = []
         for kb in range(K_BLOCKS):
             early_w.append(held.tile([P, len(EARLY) * H], BF16, name=f"early_w{kb}"))
-            queue = nc.sync if kb % 2 == 0 else nc.scalar
-            queue.dma_start(early_w[kb][:], weights_hbm[kb][:, 0 : len(EARLY) * H])
+            nc.sync.dma_start(early_w[kb][:], weights_hbm[kb][:, 0 : len(EARLY) * H])
         cell_sb = held.tile([P, CB, N], F32, name="cell_sb")
         nc.sync.dma_start(cell_sb[:], cell.rearrange("(cb p) j -> p cb j", p=P))
         late_w = []
-        for pair, pair_hbm in enumerate(weights_hbm_pairs):
-            late_pair = held.tile([P, 2, H], BF16, name=f"late_pair{pair}")
-            nc.sync.dma_start(late_pair[:], pair_hbm[:, :, GATE_O * H : (GATE_O + 1) * H])
-            late_w.append(late_pair[:, 0, :])
-            late_w.append(late_pair[:, 1, :])
+        for kb in range(K_BLOCKS):
+            late_w.append(held.tile([P, H], BF16, name=f"late_w{kb}"))
+            nc.sync.dma_start(late_w[kb][:], weights_hbm[kb][:, GATE_O * H : (GATE_O + 1) * H])
         windows = []
         for cb in range(CB):
             windows.append(held.tile([P, S], F32, name=f"window{cb}"))
@@ -67,31 +61,29 @@ def tile_outputdecoder_kernel(tc, base, x0, h, cell, wi, wh, b, offs, out):
         bias = held.tile([P, 4 * CB], F32, name="bias")
         nc.vector.tensor_copy(bias[:], bias_ps[:, 0 : 4 * CB])
 
-        z = [psum.tile([P, CB, N], F32, name=f"z{gate}") for gate in range(4)]
+        z_early = [psum.tile([P, CB, N], F32, name=f"z_early{gate}") for gate in EARLY]
+        z_late = [psum.tile([P, N], F32, name=f"z_late{cb}") for cb in range(CB)]
 
-        def accumulate(gate, kb, weights_sb, first_column):
-            for cb in range(CB):
-                nc.tensor.matmul(
-                    z[gate][:, cb, :],
-                    weights_sb[:, first_column + cb * P : first_column + (cb + 1) * P],
-                    moving_sb[kb],
-                    start=(kb == 0 and cb == 0),
-                    stop=(kb == K_BLOCKS - 1 and cb == CB - 1),
-                )
-
-        def squash(gate, cb, func, label):
+        def squash(z_block, gate, cb, func, label):
             squashed = held.tile([P, N], F32, name=f"{label}{cb}")
             column = gate * CB + cb
-            nc.scalar.activation(squashed[:], z[gate][:, cb, :], func, bias=bias[:, column : column + 1])
+            nc.scalar.activation(squashed[:], z_block, func, bias=bias[:, column : column + 1])
             return squashed
 
         for kb in range(K_BLOCKS):
             for gate in EARLY:
-                accumulate(gate, kb, early_w[kb], gate * H)
+                for cb in range(CB):
+                    nc.tensor.matmul(
+                        z_early[gate][:, cb, :],
+                        early_w[kb][:, gate * H + cb * P : gate * H + (cb + 1) * P],
+                        moving_sb[kb],
+                        start=(kb == 0 and cb == 0),
+                        stop=(kb == K_BLOCKS - 1 and cb == CB - 1),
+                    )
 
-        sig_i = [squash(GATE_I, cb, SIGMOID, "sig_i") for cb in range(CB)]
-        sig_f = [squash(GATE_F, cb, SIGMOID, "sig_f") for cb in range(CB)]
-        tanh_u = [squash(GATE_U, cb, TANH, "tanh_u") for cb in range(CB)]
+        sig_i = [squash(z_early[GATE_I][:, cb, :], GATE_I, cb, SIGMOID, "sig_i") for cb in range(CB)]
+        sig_f = [squash(z_early[GATE_F][:, cb, :], GATE_F, cb, SIGMOID, "sig_f") for cb in range(CB)]
+        tanh_u = [squash(z_early[GATE_U][:, cb, :], GATE_U, cb, TANH, "tanh_u") for cb in range(CB)]
 
         tanh_cn = []
         for cb in range(CB):
@@ -104,10 +96,22 @@ def tile_outputdecoder_kernel(tc, base, x0, h, cell, wi, wh, b, offs, out):
             tanh_cn.append(held.tile([P, N], F32, name=f"tanh_cn{cb}"))
             nc.scalar.activation(tanh_cn[cb][:], cn[:], TANH)
 
-        for kb in range(K_BLOCKS):
-            accumulate(GATE_O, kb, late_w[kb], 0)
+        def accumulate_late(kb, cb):
+            nc.tensor.matmul(
+                z_late[cb][:],
+                late_w[kb][:, cb * P : (cb + 1) * P],
+                moving_sb[kb],
+                start=(kb == 0),
+                stop=(kb == K_BLOCKS - 1),
+            )
+
+        for kb in range(K_BLOCKS // 2):
+            for cb in range(CB):
+                accumulate_late(kb, cb)
 
         for cb in range(CB):
-            sig_o = squash(GATE_O, cb, SIGMOID, "sig_o")
+            for kb in range(K_BLOCKS // 2, K_BLOCKS):
+                accumulate_late(kb, cb)
+            sig_o = squash(z_late[cb][:], GATE_O, cb, SIGMOID, "sig_o")
             nc.vector.tensor_tensor(windows[cb][:].indirect(offsets[:]), sig_o[:], tanh_cn[cb][:], MULT)
             nc.sync.dma_start(out[cb * P : (cb + 1) * P, :], windows[cb][:])

@@ -20,9 +20,6 @@ FLOPS = 2 * (768 + 512) * 4 * H * N
 def tile_outputdecoder_kernel(tc, base, x0, h, cell, wi, wh, b, offs, out):
     nc = tc.nc
     with tc.tile_pool(name="held", bufs=1) as held, tc.psum_pool(name="psum", bufs=1) as psum:
-        offsets = held.tile([P, N // 16], U16, name="offsets")
-        nc.sync.dma_start(offsets[:], offs)
-
         weights_hbm = []
         moving_sb = []
         for label, weights, moving in (("x", wi, x0), ("h", wh, h)):
@@ -49,6 +46,8 @@ def tile_outputdecoder_kernel(tc, base, x0, h, cell, wi, wh, b, offs, out):
         for kb in range(K_BLOCKS):
             late_w.append(held.tile([P, H], BF16, name=f"late_w{kb}"))
             nc.sync.dma_start(late_w[kb][:], weights_hbm[kb][:, GATE_O * H : (GATE_O + 1) * H])
+        offsets = held.tile([P, N // 16], U16, name="offsets")
+        nc.sync.dma_start(offsets[:], offs)
         windows = []
         for cb in range(CB):
             windows.append(held.tile([P, S], F32, name=f"window{cb}"))
@@ -85,16 +84,14 @@ def tile_outputdecoder_kernel(tc, base, x0, h, cell, wi, wh, b, offs, out):
         sig_f = [squash(z_early[GATE_F][:, cb, :], GATE_F, cb, SIGMOID, "sig_f") for cb in range(CB)]
         tanh_u = [squash(z_early[GATE_U][:, cb, :], GATE_U, cb, TANH, "tanh_u") for cb in range(CB)]
 
-        tanh_cn = []
+        cn = []
         for cb in range(CB):
             kept = held.tile([P, N], F32, name=f"kept{cb}")
             nc.vector.tensor_tensor(kept[:], sig_f[cb][:], cell_sb[:, cb, :], MULT)
             fresh = held.tile([P, N], F32, name=f"fresh{cb}")
             nc.vector.tensor_tensor(fresh[:], sig_i[cb][:], tanh_u[cb][:], MULT)
-            cn = held.tile([P, N], F32, name=f"cn{cb}")
-            nc.vector.tensor_tensor(cn[:], kept[:], fresh[:], ADD)
-            tanh_cn.append(held.tile([P, N], F32, name=f"tanh_cn{cb}"))
-            nc.scalar.activation(tanh_cn[cb][:], cn[:], TANH)
+            cn.append(held.tile([P, N], F32, name=f"cn{cb}"))
+            nc.vector.tensor_tensor(cn[cb][:], kept[:], fresh[:], ADD)
 
         def accumulate_late(kb, cb):
             nc.tensor.matmul(
@@ -105,13 +102,13 @@ def tile_outputdecoder_kernel(tc, base, x0, h, cell, wi, wh, b, offs, out):
                 stop=(kb == K_BLOCKS - 1),
             )
 
-        for kb in range(K_BLOCKS // 2):
+        for kb in range(K_BLOCKS):
             for cb in range(CB):
                 accumulate_late(kb, cb)
 
         for cb in range(CB):
-            for kb in range(K_BLOCKS // 2, K_BLOCKS):
-                accumulate_late(kb, cb)
+            tanh_cn = held.tile([P, N], F32, name=f"tanh_cn{cb}")
+            nc.scalar.activation(tanh_cn[:], cn[cb][:], TANH)
             sig_o = squash(z_late[cb][:], GATE_O, cb, SIGMOID, "sig_o")
-            nc.vector.tensor_tensor(windows[cb][:].indirect(offsets[:]), sig_o[:], tanh_cn[cb][:], MULT)
+            nc.vector.tensor_tensor(windows[cb][:].indirect(offsets[:]), sig_o[:], tanh_cn[:], MULT)
             nc.sync.dma_start(out[cb * P : (cb + 1) * P, :], windows[cb][:])

@@ -20,32 +20,42 @@ FLOPS = 2 * (768 + 512) * 4 * H * N
 def tile_outputdecoder_kernel(tc, base, x0, h, cell, wi, wh, b, offs, out):
     nc = tc.nc
     with tc.tile_pool(name="held", bufs=1) as held, tc.psum_pool(name="psum", bufs=1) as psum:
-        weights_hbm = []
-        moving_sb = []
-        for label, weights, moving in (("x", wi, x0), ("h", wh, h)):
+        def load_moving(label, moving):
             blocks = moving.shape[0] // P
             moving_tile = held.tile([P, blocks, N], BF16, name=f"moving_{label}")
             nc.sync.dma_start(moving_tile[:], moving.rearrange("(p kb) j -> p kb j", kb=blocks))
+            return [moving_tile[:, kb, :] for kb in range(blocks)]
+
+        def rows_of(weights):
+            blocks = weights.shape[0] // P
             weights_view = weights.rearrange("(p kb) m -> p kb m", kb=blocks)
-            for kb in range(blocks):
-                weights_hbm.append(weights_view[:, kb, :])
-                moving_sb.append(moving_tile[:, kb, :])
-        K_BLOCKS = len(weights_hbm)
+            return [weights_view[:, kb, :] for kb in range(blocks)]
 
         bias_rows = held.tile([P, P], F32, name="bias_rows")
         nc.vector.memset(bias_rows[:], 0.0)
         nc.scalar.dma_start(bias_rows[0 : 4 * CB, :], b.rearrange("(r p) one -> r (p one)", p=P))
 
         early_w = []
-        for kb in range(K_BLOCKS):
-            early_w.append(held.tile([P, len(EARLY) * H], BF16, name=f"early_w{kb}"))
-            nc.sync.dma_start(early_w[kb][:], weights_hbm[kb][:, 0 : len(EARLY) * H])
+        late_w = []
+        moving_sb = load_moving("h", h)
+        for kb, rows in enumerate(rows_of(wh)):
+            whole_w = held.tile([P, 4 * H], BF16, name=f"whole_w{kb}")
+            nc.sync.dma_start(whole_w[:], rows)
+            early_w.append(whole_w[:, 0 : len(EARLY) * H])
+            late_w.append(whole_w[:, GATE_O * H : (GATE_O + 1) * H])
+        WHOLE = len(early_w)
+        moving_sb += load_moving("x", x0)
+        for kb, rows in enumerate(rows_of(wi)):
+            split_early = held.tile([P, len(EARLY) * H], BF16, name=f"split_early{kb}")
+            nc.sync.dma_start(split_early[:], rows[:, 0 : len(EARLY) * H])
+            early_w.append(split_early[:])
         cell_sb = held.tile([P, CB, N], F32, name="cell_sb")
         nc.sync.dma_start(cell_sb[:], cell.rearrange("(cb p) j -> p cb j", p=P))
-        late_w = []
-        for kb in range(K_BLOCKS):
-            late_w.append(held.tile([P, H], BF16, name=f"late_w{kb}"))
-            nc.sync.dma_start(late_w[kb][:], weights_hbm[kb][:, GATE_O * H : (GATE_O + 1) * H])
+        for kb, rows in enumerate(rows_of(wi)):
+            split_late = held.tile([P, H], BF16, name=f"split_late{kb}")
+            nc.sync.dma_start(split_late[:], rows[:, GATE_O * H : (GATE_O + 1) * H])
+            late_w.append(split_late[:])
+        K_BLOCKS = len(early_w)
         offsets = held.tile([P, N // 16], U16, name="offsets")
         nc.sync.dma_start(offsets[:], offs)
         windows = []
@@ -69,6 +79,16 @@ def tile_outputdecoder_kernel(tc, base, x0, h, cell, wi, wh, b, offs, out):
             nc.scalar.activation(squashed[:], z_block, func, bias=bias[:, column : column + 1])
             return squashed
 
+        def accumulate_late(kb):
+            for cb in range(CB):
+                nc.tensor.matmul(
+                    z_late[cb][:],
+                    late_w[kb][:, cb * P : (cb + 1) * P],
+                    moving_sb[kb],
+                    start=(kb == 0),
+                    stop=(kb == K_BLOCKS - 1),
+                )
+
         for kb in range(K_BLOCKS):
             for gate in EARLY:
                 for cb in range(CB):
@@ -79,6 +99,8 @@ def tile_outputdecoder_kernel(tc, base, x0, h, cell, wi, wh, b, offs, out):
                         start=(kb == 0 and cb == 0),
                         stop=(kb == K_BLOCKS - 1 and cb == CB - 1),
                     )
+            if kb < WHOLE:
+                accumulate_late(kb)
 
         sig_i = [squash(z_early[GATE_I][:, cb, :], GATE_I, cb, SIGMOID, "sig_i") for cb in range(CB)]
         sig_f = [squash(z_early[GATE_F][:, cb, :], GATE_F, cb, SIGMOID, "sig_f") for cb in range(CB)]
@@ -93,18 +115,8 @@ def tile_outputdecoder_kernel(tc, base, x0, h, cell, wi, wh, b, offs, out):
             cn.append(held.tile([P, N], F32, name=f"cn{cb}"))
             nc.vector.tensor_tensor(cn[cb][:], kept[:], fresh[:], ADD)
 
-        def accumulate_late(kb, cb):
-            nc.tensor.matmul(
-                z_late[cb][:],
-                late_w[kb][:, cb * P : (cb + 1) * P],
-                moving_sb[kb],
-                start=(kb == 0),
-                stop=(kb == K_BLOCKS - 1),
-            )
-
-        for kb in range(K_BLOCKS):
-            for cb in range(CB):
-                accumulate_late(kb, cb)
+        for kb in range(WHOLE, K_BLOCKS):
+            accumulate_late(kb)
 
         for cb in range(CB):
             tanh_cn = held.tile([P, N], F32, name=f"tanh_cn{cb}")

@@ -90,7 +90,7 @@ def tile_outputdecoder_kernel(tc, base, x0, h, cell, wi, wh, b, offs, out):
                 )
 
         for kb in range(K_BLOCKS):
-            for gate in EARLY:
+            for gate in (GATE_F, GATE_I, GATE_U):
                 for cb in range(CB):
                     nc.tensor.matmul(
                         z_early[gate][:, cb, :],
@@ -102,18 +102,19 @@ def tile_outputdecoder_kernel(tc, base, x0, h, cell, wi, wh, b, offs, out):
             if kb < WHOLE:
                 accumulate_late(kb)
 
-        sig_i = [squash(z_early[GATE_I][:, cb, :], GATE_I, cb, SIGMOID, "sig_i") for cb in range(CB)]
-        sig_f = [squash(z_early[GATE_F][:, cb, :], GATE_F, cb, SIGMOID, "sig_f") for cb in range(CB)]
-        tanh_u = [squash(z_early[GATE_U][:, cb, :], GATE_U, cb, TANH, "tanh_u") for cb in range(CB)]
-
+        kept = []
+        for cb in range(CB):
+            sig_f = squash(z_early[GATE_F][:, cb, :], GATE_F, cb, SIGMOID, "sig_f")
+            kept.append(held.tile([P, N], F32, name=f"kept{cb}"))
+            nc.vector.tensor_tensor(kept[cb][:], sig_f[:], cell_sb[:, cb, :], MULT)
         cn = []
         for cb in range(CB):
-            kept = held.tile([P, N], F32, name=f"kept{cb}")
-            nc.vector.tensor_tensor(kept[:], sig_f[cb][:], cell_sb[:, cb, :], MULT)
+            sig_i = squash(z_early[GATE_I][:, cb, :], GATE_I, cb, SIGMOID, "sig_i")
+            tanh_u = squash(z_early[GATE_U][:, cb, :], GATE_U, cb, TANH, "tanh_u")
             fresh = held.tile([P, N], F32, name=f"fresh{cb}")
-            nc.vector.tensor_tensor(fresh[:], sig_i[cb][:], tanh_u[cb][:], MULT)
+            nc.vector.tensor_tensor(fresh[:], sig_i[:], tanh_u[:], MULT)
             cn.append(held.tile([P, N], F32, name=f"cn{cb}"))
-            nc.vector.tensor_tensor(cn[cb][:], kept[:], fresh[:], ADD)
+            nc.vector.tensor_tensor(cn[cb][:], kept[cb][:], fresh[:], ADD)
 
         for kb in range(WHOLE, K_BLOCKS):
             accumulate_late(kb)

import concourse.masks as masks
import concourse.mybir as mybir

BF16, F32, U16 = mybir.dt.bfloat16, mybir.dt.float32, mybir.dt.uint16
SIGMOID = mybir.ActivationFunctionType.Sigmoid
TANH = mybir.ActivationFunctionType.Tanh
MULT, ADD = mybir.AluOpType.mult, mybir.AluOpType.add

P = 128
H = 512
N = 128
S = 512
CB = H // P
GATE_I, GATE_F, GATE_U, GATE_O = 0, 1, 2, 3
EARLY = (GATE_I, GATE_F, GATE_U)

FLOPS = 2 * (768 + 512) * 4 * H * N


def tile_outputdecoder_kernel(tc, base, x0, h, cell, wi, wh, b, offs, out):
    nc = tc.nc
    with tc.tile_pool(name="held", bufs=1) as held, tc.psum_pool(name="psum", bufs=1) as psum:
        def load_moving(label, moving):
            blocks = moving.shape[0] // P
            moving_tile = held.tile([P, blocks, N], BF16, name=f"moving_{label}")
            nc.sync.dma_start(moving_tile[:], moving.rearrange("(p kb) j -> p kb j", kb=blocks))
            return [moving_tile[:, kb, :] for kb in range(blocks)]

        def rows_of(weights):
            blocks = weights.shape[0] // P
            weights_view = weights.rearrange("(p kb) m -> p kb m", kb=blocks)
            return [weights_view[:, kb, :] for kb in range(blocks)]

        bias_rows = held.tile([P, P], F32, name="bias_rows")
        nc.vector.memset(bias_rows[:], 0.0)
        nc.scalar.dma_start(bias_rows[0 : 4 * CB, :], b.rearrange("(r p) one -> r (p one)", p=P))

        early_w = []
        late_w = []
        moving_sb = load_moving("h", h)
        for kb, rows in enumerate(rows_of(wh)):
            whole_w = held.tile([P, 4 * H], BF16, name=f"whole_w{kb}")
            nc.sync.dma_start(whole_w[:], rows)
            early_w.append(whole_w[:, 0 : len(EARLY) * H])
            late_w.append(whole_w[:, GATE_O * H : (GATE_O + 1) * H])
        WHOLE = len(early_w)
        moving_sb += load_moving("x", x0)
        for kb, rows in enumerate(rows_of(wi)):
            split_early = held.tile([P, len(EARLY) * H], BF16, name=f"split_early{kb}")
            nc.sync.dma_start(split_early[:], rows[:, 0 : len(EARLY) * H])
            early_w.append(split_early[:])
        cell_sb = held.tile([P, CB, N], F32, name="cell_sb")
        nc.sync.dma_start(cell_sb[:], cell.rearrange("(cb p) j -> p cb j", p=P))
        for kb, rows in enumerate(rows_of(wi)):
            split_late = held.tile([P, H], BF16, name=f"split_late{kb}")
            nc.sync.dma_start(split_late[:], rows[:, GATE_O * H : (GATE_O + 1) * H])
            late_w.append(split_late[:])
        K_BLOCKS = len(early_w)
        offsets = held.tile([P, N // 16], U16, name="offsets")
        nc.sync.dma_start(offsets[:], offs)
        windows = []
        for cb in range(CB):
            windows.append(held.tile([P, S], F32, name=f"window{cb}"))
            nc.sync.dma_start(windows[cb][:], base[cb * P : (cb + 1) * P, :])

        identity = held.tile([P, P], F32, name="identity")
        masks.make_identity(nc, identity[:])
        bias_ps = psum.tile([P, P], F32, name="bias_ps")
        nc.tensor.transpose(bias_ps[:], bias_rows[:], identity[:])
        bias = held.tile([P, 4 * CB], F32, name="bias")
        nc.vector.tensor_copy(bias[:], bias_ps[:, 0 : 4 * CB])

        z_early = [psum.tile([P, CB, N], F32, name=f"z_early{gate}") for gate in EARLY]
        z_late = [psum.tile([P, N], F32, name=f"z_late{cb}") for cb in range(CB)]

        def squash(z_block, gate, cb, func, label):
            squashed = held.tile([P, N], F32, name=f"{label}{cb}")
            column = gate * CB + cb
            nc.scalar.activation(squashed[:], z_block, func, bias=bias[:, column : column + 1])
            return squashed

        def accumulate_late(kb):
            for cb in range(CB):
                nc.tensor.matmul(
                    z_late[cb][:],
                    late_w[kb][:, cb * P : (cb + 1) * P],
                    moving_sb[kb],
                    start=(kb == 0),
                    stop=(kb == K_BLOCKS - 1),
                )

        for kb in range(K_BLOCKS):
            for gate in (GATE_F, GATE_I, GATE_U):
                for cb in range(CB):
                    nc.tensor.matmul(
                        z_early[gate][:, cb, :],
                        early_w[kb][:, gate * H + cb * P : gate * H + (cb + 1) * P],
                        moving_sb[kb],
                        start=(kb == 0 and cb == 0),
                        stop=(kb == K_BLOCKS - 1 and cb == CB - 1),
                    )
            if kb < WHOLE:
                accumulate_late(kb)

        kept = []
        for cb in range(CB):
            sig_f = squash(z_early[GATE_F][:, cb, :], GATE_F, cb, SIGMOID, "sig_f")
            kept.append(held.tile([P, N], F32, name=f"kept{cb}"))
            nc.vector.tensor_tensor(kept[cb][:], sig_f[:], cell_sb[:, cb, :], MULT)
        cn = []
        for cb in range(CB):
            sig_i = squash(z_early[GATE_I][:, cb, :], GATE_I, cb, SIGMOID, "sig_i")
            tanh_u = squash(z_early[GATE_U][:, cb, :], GATE_U, cb, TANH, "tanh_u")
            fresh = held.tile([P, N], F32, name=f"fresh{cb}")
            nc.vector.tensor_tensor(fresh[:], sig_i[:], tanh_u[:], MULT)
            cn.append(held.tile([P, N], F32, name=f"cn{cb}"))
            nc.vector.tensor_tensor(cn[cb][:], kept[cb][:], fresh[:], ADD)

        for kb in range(WHOLE, K_BLOCKS):
            accumulate_late(kb)

        for cb in range(CB):
            tanh_cn = held.tile([P, N], F32, name=f"tanh_cn{cb}")
            nc.scalar.activation(tanh_cn[:], cn[cb][:], TANH)
            sig_o = squash(z_late[cb][:], GATE_O, cb, SIGMOID, "sig_o")
            nc.vector.tensor_tensor(windows[cb][:].indirect(offsets[:]), sig_o[:], tanh_cn[:], MULT)
            nc.sync.dma_start(out[cb * P : (cb + 1) * P, :], windows[cb][:])
